import numpy as np
import ml_dtypes


def mxq(x, axis, fmt="e4m3"):
    dtype, down = {"e4m3": (ml_dtypes.float8_e4m3fn, 7), "e5m2": (ml_dtypes.float8_e5m2, 14)}[fmt]
    v = np.moveaxis(np.asarray(x, np.float32).astype(ml_dtypes.bfloat16).astype(np.float64), axis, -1)
    blocks = v.reshape(v.shape[:-1] + (-1, 32))
    amax = np.abs(blocks).max(-1, keepdims=True)
    byte = np.maximum(np.where(amax > 0, np.frexp(amax)[1] - 1 + 127, 0) - down, 1)
    scale = np.exp2(byte - 127.0)
    codes = (blocks / scale).astype(np.float32).astype(dtype).astype(np.float64)
    return np.moveaxis((codes * scale).reshape(v.shape), -1, axis)


WIDE = False


def mx_kscale(k):
    if not WIDE:
        return np.ones(k)
    levels = np.array([10, -10, 5, -5, 0])
    if k % 512:
        return np.exp2(np.random.permutation(np.resize(levels, k // 32))).repeat(32)
    a = np.empty((k // 512, 16))
    for p in range(k // 512):
        a[p, :8] = np.random.permutation(np.resize(levels, 8))
        for g in range(8):
            far = levels[np.abs(levels - a[p, g]) >= 10]
            a[p, g + 8] = far[np.random.randint(len(far))]
    return np.exp2(a.ravel()).repeat(32)


BF16 = ml_dtypes.bfloat16


def bf(x):
    return np.asarray(x, np.float32).astype(BF16)


def f64(x):
    return np.asarray(x).astype(np.float64)


B, S, D, H = 8, 1024, 1024, 2


def setup_inputs():
    s = mx_kscale(D)
    t = np.tile(mx_kscale(D), H)
    return {"x": bf(np.random.standard_normal((B, S, D)) * s),
            "Wq": bf(np.random.standard_normal((D, H * D)) * 1.4 / np.sqrt(D) / s[:, None] * t),
            "Wk": bf(np.random.standard_normal((D, H * D)) * 1.4 / np.sqrt(D) / s[:, None] / t)}


def reference(x, Wq, Wk):
    xq = mxq(f64(x), 2, "e4m3")
    Q = np.reshape(xq @ mxq(f64(Wq), 0, "e4m3"), (B, H, S, D))
    K = np.reshape(xq @ mxq(f64(Wk), 0, "e4m3"), (B, H, S, D))
    scores = mxq(Q, 3, "e4m3") @ mxq(K, 3, "e4m3").transpose(0, 1, 3, 2)
    z = scores / np.sqrt(D)
    e = np.exp(z - z.max(-1, keepdims=True))
    return e / e.sum(-1, keepdims=True)

@@ -1,0 +1,345 @@
+from contextlib import ExitStack
+
+import concourse.mybir as mybir
+from concourse.masks import make_identity
+
+B, S, D, H = 8, 1024, 1024, 2
+FLOPS = 2 * B * S * D * (2 * H * D) + 2 * B * H * S * S * D
+
+F32 = mybir.dt.float32
+BF16 = mybir.dt.bfloat16
+U32 = mybir.dt.uint32
+U8 = mybir.dt.uint8
+FP8X4 = mybir.dt.float8_e4m3fn_x4
+ALU = mybir.AluOpType
+ACT = mybir.ActivationFunctionType
+AXIS_X = mybir.AxisListType.X
+
+UNITS = B * H
+SLOTS = 8
+Q_MAT, K_MAT = 0, 1
+
+
+def unit_combos():
+    combos = []
+    for g in range(2):
+        for tb in range(2):
+            banks = [(2 * half + g, 2 * tb + sub, 256 * half + 128 * sub) for half in range(2) for sub in range(2)]
+            combos.append((K_MAT, g, tb, banks))
+    for hq in range(2):
+        for g in range(2):
+            banks = [(2 * hq + g, nb, 128 * nb) for nb in range(4)]
+            combos.append((Q_MAT, g, hq, banks))
+    return combos
+
+
+def weight_pieces():
+    pieces = []
+    for grp in (0, 2, 1, 3):
+        for kp in range(2):
+            pieces.append((K_MAT, grp, kp))
+    for grp in range(4):
+        for kp in range(2):
+            pieces.append((Q_MAT, grp, kp))
+    return pieces
+
+
+def tile_bertselfattention_pa_l_kernel(tc, x, Wq, Wk, out):
+    nc = tc.nc
+    weights = (Wq, Wk)
+    combos = unit_combos()
+    pieces = weight_pieces()
+
+    with ExitStack() as ctx:
+        keep = ctx.enter_context(tc.tile_pool(name="keep", bufs=1))
+        wraw_pool = ctx.enter_context(tc.tile_pool(name="wraw", bufs=8))
+        xraw_pool = ctx.enter_context(tc.tile_pool(name="xraw", bufs=3))
+        xg_pool = ctx.enter_context(tc.tile_pool(name="xg", bufs=2))
+        xc_pool = ctx.enter_context(tc.tile_pool(name="xc", bufs=2))
+        gr_pool = ctx.enter_context(tc.tile_pool(name="gr", bufs=6))
+        qk_pool = ctx.enter_context(tc.tile_pool(name="qk", bufs=2))
+        e_pool = ctx.enter_context(tc.tile_pool(name="e", bufs=4))
+        o_pool = ctx.enter_context(tc.tile_pool(name="o", bufs=4))
+        st_pool = ctx.enter_context(tc.tile_pool(name="st", bufs=6))
+        ps1 = ctx.enter_context(tc.psum_pool(name="ps1", bufs=4))
+        ps2 = ctx.enter_context(tc.psum_pool(name="ps2", bufs=4))
+        ctx.enter_context(tc.manual_schedule())
+
+        ident = keep.tile([128, 128], F32, name="ident")
+        make_identity(nc, ident[:])
+        warm_in = keep.tile([128, 1], F32, name="warm_in")
+        warm_out = keep.tile([128, 1], F32, name="warm_out")
+        nc.vector.memset(warm_in[:], 0.0)
+        nc.scalar.activation(out=warm_out[:], in_=warm_in[:], func=ACT.Exp)
+
+        w_codes = {}
+        w_scales = {}
+        for piece in pieces:
+            w_codes[piece] = keep.tile([128, 512], U32, name="wc%d%d%d" % piece, align_bytes=64)
+            w_scales[piece] = keep.tile([128, 512], U8, name="ws%d%d%d" % piece, align_bytes=64)
+
+        w_raw = {}
+        w_grouped = {}
+        x_raw = {}
+        x_grouped = {}
+        x_codes = {}
+        x_scales = {}
+        qk_codes = {}
+        qk_scales = {}
+        banks_of = {}
+        grouped_of = {}
+        scores_of = {}
+        stats_of = {}
+        exp_of = {}
+
+        def load_w(i):
+            m, grp, kp = pieces[i]
+            raw = wraw_pool.tile([128, 4, 512], BF16, name="wr")
+            src = weights[m][512 * kp : 512 * (kp + 1), 512 * grp : 512 * (grp + 1)]
+            nc.sync.dma_start(out=raw[:], in_=src.rearrange("(p j) c -> p j c", j=4))
+            w_raw[i] = raw
+
+        def interleave_w(copy, i):
+            grouped = gr_pool.tile([128, 2048], BF16, name="gr", align_bytes=64)
+            copy(
+                out=grouped[:].rearrange("p (t m j) -> p t m j", t=4, j=4),
+                in_=w_raw[i][:].rearrange("p j (m t) -> p t m j", t=4),
+            )
+            w_grouped[i] = grouped
+
+        def quantize_w(i):
+            nc.vector.quantize_mx(
+                out=w_codes[pieces[i]][:].bitcast(FP8X4), scales=w_scales[pieces[i]][:], in_=w_grouped[i][:]
+            )
+
+        def load_x(u):
+            b, h = divmod(u, H)
+            raw = xraw_pool.tile([128, 4, D], BF16, name="xr")
+            src = x[b, 512 * h : 512 * (h + 1), :].rearrange("(n p) d -> p n d", p=128)
+            for part in range(2):
+                nc.sync.dma_start(out=raw[:, 2 * part : 2 * part + 2, :], in_=src[:, 2 * part : 2 * part + 2, :])
+            x_raw[u] = raw
+
+        def transpose_x(u, n):
+            bank = ps1.tile([128, 512], F32, name="bank")
+            words = x_raw[u][:, n, :].bitcast(F32)
+            for g in range(2):
+                for w in range(2):
+                    c0 = 128 * (2 * g + w)
+                    nc.tensor.transpose(bank[:, c0 : c0 + 128], words[:, 256 * g + w : 256 * (g + 1) : 2], ident[:])
+            return bank
+
+        def evac_x(copy, u, n, bank):
+            if n == 0:
+                x_grouped[u] = xg_pool.tile([128, 4096], BF16, name="xg", align_bytes=64)
+            dst = x_grouped[u][:].bitcast(F32).rearrange("p (g r w) -> p g r w", g=2, w=2)
+            copy(out=dst[:, :, 128 * n : 128 * (n + 1), :], in_=bank[:].rearrange("p (g w r) -> p g r w", g=2, w=2))
+
+        def quantize_x(u, g):
+            x_codes[(u, g)] = xc_pool.tile([128, 512], U32, name="xc%d" % g, align_bytes=64)
+            x_scales[(u, g)] = xc_pool.tile([128, 512], U8, name="xs%d" % g, align_bytes=64)
+            nc.vector.quantize_mx(
+                out=x_codes[(u, g)][:].bitcast(FP8X4),
+                scales=x_scales[(u, g)][:],
+                in_=x_grouped[u][:, 2048 * g : 2048 * (g + 1)],
+            )
+
+        def has_combo(sg):
+            return 0 <= sg < SLOTS * UNITS
+
+        def project(sg, k):
+            u, s = divmod(sg, SLOTS)
+            m, g, part, banks = combos[s]
+            grp, nb, off = banks[k]
+            bank = ps1.tile([128, 512], F32, name="bank")
+            toks = slice(128 * nb, 128 * (nb + 1))
+            for t in range(4):
+                cols = slice(128 * t, 128 * (t + 1))
+                for kp in range(2):
+                    nc.tensor.matmul_mx(
+                        out=bank[:, cols],
+                        lhsT=w_codes[(m, grp, kp)][:, cols].bitcast(FP8X4),
+                        lhsT_scale=w_scales[(m, grp, kp)][:, cols],
+                        rhs=x_codes[(u, kp)][:, toks].bitcast(FP8X4),
+                        rhs_scale=x_scales[(u, kp)][:, toks],
+                        start=(kp == 0),
+                        stop=(kp == 1),
+                    )
+            banks_of[(sg, k)] = bank
+
+        def evac_proj(copy, sg, k):
+            off = combos[sg % SLOTS][3][k][2]
+            if k == 0:
+                grouped_of[sg] = gr_pool.tile([128, 2048], BF16, name="gr", align_bytes=64)
+            copy(
+                out=grouped_of[sg][:, 4 * off : 4 * (off + 128)].rearrange("p (r t) -> p r t", t=4),
+                in_=banks_of[(sg, k)][:].rearrange("p (t r) -> p r t", t=4),
+            )
+
+        def quantize_qk(sg):
+            u, s = divmod(sg, SLOTS)
+            m, g, part, banks = combos[s]
+            key = (u, m, g, part)
+            qk_codes[key] = qk_pool.tile([128, 512], U32, name="qkc%d%d%d" % (m, g, part), align_bytes=64)
+            qk_scales[key] = qk_pool.tile([128, 512], U8, name="qks%d%d%d" % (m, g, part), align_bytes=64)
+            nc.vector.quantize_mx(out=qk_codes[key][:].bitcast(FP8X4), scales=qk_scales[key][:], in_=grouped_of[sg][:])
+
+        def has_rows(sg):
+            return SLOTS <= sg < SLOTS * (UNITS + 1)
+
+        def scores(sg):
+            u, s = divmod(sg - SLOTS, SLOTS)
+            hq, tq = divmod(s, 4)
+            rows = slice(128 * tq, 128 * (tq + 1))
+            pair = []
+            for tb in range(2):
+                ps = ps2.tile([128, 512], F32, name="sc")
+                for g in range(2):
+                    nc.tensor.matmul_mx(
+                        out=ps[:],
+                        lhsT=qk_codes[(u, Q_MAT, g, hq)][:, rows].bitcast(FP8X4),
+                        lhsT_scale=qk_scales[(u, Q_MAT, g, hq)][:, rows],
+                        rhs=qk_codes[(u, K_MAT, g, tb)][:].bitcast(FP8X4),
+                        rhs_scale=qk_scales[(u, K_MAT, g, tb)][:],
+                        start=(g == 0),
+                        stop=(g == 1),
+                    )
+                pair.append(ps)
+            scores_of[sg] = pair
+
+        def row_max(sg):
+            mx = st_pool.tile([128, 2], F32, name="mx")
+            for tb in range(2):
+                nc.vector.tensor_reduce(out=mx[:, tb : tb + 1], in_=scores_of[sg][tb][:], axis=AXIS_X, op=ALU.max)
+            stats_of[(sg, "mx")] = mx
+
+        def neg_max(sg):
+            mx = stats_of[(sg, "mx")]
+            nb = st_pool.tile([128, 1], F32, name="nb")
+            nc.vector.tensor_scalar(
+                out=nb[:], in0=mx[:, 0:1], scalar1=mx[:, 1:2], scalar2=-1.0 / 32.0, op0=ALU.max, op1=ALU.mult
+            )
+            stats_of[(sg, "nb")] = nb
+
+        def exps(sg):
+            e = e_pool.tile([128, 1024], F32, name="e")
+            ss = st_pool.tile([128, 2], F32, name="ss")
+            for tb in range(2):
+                nc.scalar.activation(
+                    out=e[:, 512 * tb : 512 * (tb + 1)].rearrange("p (t h) -> p t h", h=2),
+                    in_=scores_of[sg][tb][:].rearrange("p (h t) -> p t h", h=2),
+                    func=ACT.Exp,
+                    bias=stats_of[(sg, "nb")][:],
+                    scale=1.0 / 32.0,
+                    accum_out=ss[:, tb : tb + 1],
+                )
+            exp_of[sg] = e
+            stats_of[(sg, "ss")] = ss
+
+        def sum_add(sg):
+            ss = stats_of[(sg, "ss")]
+            tot = st_pool.tile([128, 1], F32, name="tot")
+            nc.vector.tensor_tensor(out=tot[:], in0=ss[:, 0:1], in1=ss[:, 1:2], op=ALU.add)
+            stats_of[(sg, "tot")] = tot
+
+        def recip(sg):
+            rc = st_pool.tile([128, 1], F32, name="rc")
+            nc.vector.reciprocal(out=rc[:], in_=stats_of[(sg, "tot")][:])
+            stats_of[(sg, "rc")] = rc
+
+        def normalise_and_store(sg):
+            u, s = divmod(sg - SLOTS, SLOTS)
+            b, h = divmod(u, H)
+            hq, tq = divmod(s, 4)
+            o = o_pool.tile([128, 1024], F32, name="o")
+            nc.vector.tensor_scalar(
+                out=o[:], in0=exp_of[sg][:], scalar1=stats_of[(sg, "rc")][:], scalar2=None, op0=ALU.mult
+            )
+            dst = out[b, h].rearrange("(t two) j -> two t j", two=2)
+            nc.sync.dma_start(out=dst[hq, 128 * tq : 128 * (tq + 1), :], in_=o[:])
+
+        vcopy = nc.vector.tensor_copy
+        scopy = nc.scalar.copy
+
+        def vector_takes_last(sg):
+            return sg % SLOTS < 6
+
+        load_x(0)
+        for i in range(4):
+            load_w(i)
+        load_x(1)
+        for i in range(4, 8):
+            load_w(i)
+
+        for n0 in (0, 2):
+            first = transpose_x(0, n0)
+            second = transpose_x(0, n0 + 1)
+            evac_x(scopy, 0, n0, first)
+            evac_x(vcopy, 0, n0 + 1, second)
+        interleave_w(vcopy, 0)
+        interleave_w(scopy, 1)
+        quantize_x(0, 0)
+        quantize_x(0, 1)
+        quantize_w(0)
+        interleave_w(vcopy, 2)
+        interleave_w(scopy, 3)
+        quantize_w(1)
+        quantize_w(2)
+        quantize_w(3)
+        for i in range(8, 12):
+            load_w(i)
+
+        for sg in range(SLOTS * (UNITS + 1) + 2):
+            it, s = divmod(sg, SLOTS)
+            head_w = it == 0 and s < 6
+            if s == 0 and it + 2 < UNITS:
+                load_x(it + 2)
+            if head_w:
+                interleave_w(vcopy, 4 + 2 * s)
+                interleave_w(scopy, 5 + 2 * s)
+                if s < 2:
+                    load_w(12 + 2 * s)
+                    load_w(13 + 2 * s)
+
+            if has_rows(sg - 2):
+                sum_add(sg - 2)
+            if has_combo(sg - 1) and vector_takes_last(sg - 1):
+                evac_proj(vcopy, sg - 1, 3)
+            if has_rows(sg - 2):
+                recip(sg - 2)
+            if has_rows(sg - 1):
+                neg_max(sg - 1)
+            if has_rows(sg - 2):
+                normalise_and_store(sg - 2)
+            if has_combo(sg - 1):
+                quantize_qk(sg - 1)
+            if head_w:
+                quantize_w(4 + 2 * s)
+            if s >= 6 and it + 1 < UNITS:
+                quantize_x(it + 1, s - 6)
+
+            if has_combo(sg):
+                project(sg, 0)
+                project(sg, 1)
+                evac_proj(scopy, sg, 0)
+            if has_rows(sg - 1):
+                exps(sg - 1)
+            if has_combo(sg):
+                evac_proj(scopy, sg, 1)
+            if has_rows(sg):
+                scores(sg)
+                row_max(sg)
+            if has_combo(sg):
+                project(sg, 2)
+                project(sg, 3)
+                evac_proj(scopy, sg, 2)
+                if not vector_takes_last(sg):
+                    evac_proj(scopy, sg, 3)
+            if s in (1, 4) and it + 1 < UNITS:
+                n0 = 0 if s == 1 else 2
+                first = transpose_x(it + 1, n0)
+                second = transpose_x(it + 1, n0 + 1)
+                evac_x(scopy, it + 1, n0, first)
+                evac_x(scopy, it + 1, n0 + 1, second)
+            if head_w:
+                quantize_w(5 + 2 * s)

@@ -24,11 +24,11 @@ def unit_combos():
     combos = []
     for g in range(2):
         for tb in range(2):
-            banks = [(2 * half + g, 2 * tb + sub, 256 * half + 128 * sub) for half in range(2) for sub in range(2)]
+            banks = [(2 * half + g, a, 256 * tb, 256 * half) for half in range(2) for a in range(2)]
             combos.append((K_MAT, g, tb, banks))
     for hq in range(2):
         for g in range(2):
-            banks = [(2 * hq + g, nb, 128 * nb) for nb in range(4)]
+            banks = [(2 * hq + g, a, 256 * th, 256 * th) for th in range(2) for a in range(2)]
             combos.append((Q_MAT, g, hq, banks))
     return combos
 
@@ -53,10 +53,11 @@ def tile_bertselfattention_pa_l_kernel(tc, x, Wq, Wk, out):
     with ExitStack() as ctx:
         keep = ctx.enter_context(tc.tile_pool(name="keep", bufs=1))
         wraw_pool = ctx.enter_context(tc.tile_pool(name="wraw", bufs=8))
-        xraw_pool = ctx.enter_context(tc.tile_pool(name="xraw", bufs=3))
+        xraw_pool = ctx.enter_context(tc.tile_pool(name="xraw", bufs=2))
         xg_pool = ctx.enter_context(tc.tile_pool(name="xg", bufs=2))
         xc_pool = ctx.enter_context(tc.tile_pool(name="xc", bufs=2))
-        gr_pool = ctx.enter_context(tc.tile_pool(name="gr", bufs=6))
+        gr_pool = ctx.enter_context(tc.tile_pool(name="gr", bufs=4))
+        hg_pool = ctx.enter_context(tc.tile_pool(name="hg", bufs=4))
         qk_pool = ctx.enter_context(tc.tile_pool(name="qk", bufs=2))
         e_pool = ctx.enter_context(tc.tile_pool(name="e", bufs=4))
         o_pool = ctx.enter_context(tc.tile_pool(name="o", bufs=4))
@@ -88,6 +89,7 @@ def tile_bertselfattention_pa_l_kernel(tc, x, Wq, Wk, out):
         qk_scales = {}
         banks_of = {}
         grouped_of = {}
+        halves_of = {}
         scores_of = {}
         stats_of = {}
         exp_of = {}
@@ -150,14 +152,14 @@ def tile_bertselfattention_pa_l_kernel(tc, x, Wq, Wk, out):
         def project(sg, k):
             u, s = divmod(sg, SLOTS)
             m, g, part, banks = combos[s]
-            grp, nb, off = banks[k]
+            grp, a, tok0, off = banks[k]
             bank = ps1.tile([128, 512], F32, name="bank")
-            toks = slice(128 * nb, 128 * (nb + 1))
-            for t in range(4):
-                cols = slice(128 * t, 128 * (t + 1))
+            toks = slice(tok0, tok0 + 256)
+            for w in range(2):
+                cols = slice(128 * (2 * a + w), 128 * (2 * a + w + 1))
                 for kp in range(2):
                     nc.tensor.matmul_mx(
-                        out=bank[:, cols],
+                        out=bank[:, 256 * w : 256 * (w + 1)],
                         lhsT=w_codes[(m, grp, kp)][:, cols].bitcast(FP8X4),
                         lhsT_scale=w_scales[(m, grp, kp)][:, cols],
                         rhs=x_codes[(u, kp)][:, toks].bitcast(FP8X4),
@@ -168,12 +170,20 @@ def tile_bertselfattention_pa_l_kernel(tc, x, Wq, Wk, out):
             banks_of[(sg, k)] = bank
 
         def evac_proj(copy, sg, k):
-            off = combos[sg % SLOTS][3][k][2]
+            grp, a, tok0, off = combos[sg % SLOTS][3][k]
             if k == 0:
-                grouped_of[sg] = gr_pool.tile([128, 2048], BF16, name="gr", align_bytes=64)
+                halves_of[sg] = hg_pool.tile([128, 2048], BF16, name="hg", align_bytes=64)
+            c0 = 1024 * a + 2 * off
             copy(
-                out=grouped_of[sg][:, 4 * off : 4 * (off + 128)].rearrange("p (r t) -> p r t", t=4),
-                in_=banks_of[(sg, k)][:].rearrange("p (t r) -> p r t", t=4),
+                out=halves_of[sg][:, c0 : c0 + 512].rearrange("p (r w) -> p r w", w=2),
+                in_=banks_of[(sg, k)][:].rearrange("p (w r) -> p r w", w=2),
+            )
+
+        def merge_pairs(sg):
+            grouped_of[sg] = gr_pool.tile([128, 2048], BF16, name="gr", align_bytes=64)
+            nc.vector.tensor_copy(
+                out=grouped_of[sg][:].bitcast(F32).rearrange("p (c a) -> p c a", a=2),
+                in_=halves_of[sg][:].bitcast(F32).rearrange("p (a c) -> p c a", a=2),
             )
 
         def quantize_qk(sg):
@@ -252,8 +262,8 @@ def tile_bertselfattention_pa_l_kernel(tc, x, Wq, Wk, out):
             b, h = divmod(u, H)
             hq, tq = divmod(s, 4)
             o = o_pool.tile([128, 1024], F32, name="o")
-            nc.vector.tensor_scalar(
-                out=o[:], in0=exp_of[sg][:], scalar1=stats_of[(sg, "rc")][:], scalar2=None, op0=ALU.mult
+            nc.gpsimd.tensor_scalar(
+                out=o[:], in0=exp_of[sg][:], scalar1=stats_of[(sg, "rc")][:], scalar2=1.0, op0=ALU.mult, op1=ALU.mult
             )
             dst = out[b, h].rearrange("(t two) j -> two t j", two=2)
             nc.sync.dma_start(out=dst[hq, 128 * tq : 128 * (tq + 1), :], in_=o[:])
@@ -262,41 +272,44 @@ def tile_bertselfattention_pa_l_kernel(tc, x, Wq, Wk, out):
         scopy = nc.scalar.copy
 
         def vector_takes_last(sg):
-            return sg % SLOTS < 6
+            return sg >= SLOTS and sg % SLOTS < 6
 
+        for i in range(2):
+            load_w(i)
         load_x(0)
-        for i in range(4):
+        for i in range(2, 4):
             load_w(i)
         load_x(1)
         for i in range(4, 8):
             load_w(i)
 
+        interleave_w(vcopy, 0)
+        interleave_w(vcopy, 1)
         for n0 in (0, 2):
             first = transpose_x(0, n0)
             second = transpose_x(0, n0 + 1)
             evac_x(scopy, 0, n0, first)
-            evac_x(vcopy, 0, n0 + 1, second)
-        interleave_w(vcopy, 0)
-        interleave_w(scopy, 1)
+            evac_x(scopy, 0, n0 + 1, second)
+        quantize_w(0)
+        quantize_w(1)
+        interleave_w(scopy, 3)
         quantize_x(0, 0)
         quantize_x(0, 1)
-        quantize_w(0)
         interleave_w(vcopy, 2)
-        interleave_w(scopy, 3)
-        quantize_w(1)
-        quantize_w(2)
-        quantize_w(3)
         for i in range(8, 12):
             load_w(i)
+        quantize_w(3)
+        quantize_w(2)
 
         for sg in range(SLOTS * (UNITS + 1) + 2):
             it, s = divmod(sg, SLOTS)
             head_w = it == 0 and s < 6
+            second_copy = scopy if s in (0, 2, 4) else vcopy
             if s == 0 and it + 2 < UNITS:
                 load_x(it + 2)
             if head_w:
                 interleave_w(vcopy, 4 + 2 * s)
-                interleave_w(scopy, 5 + 2 * s)
+                interleave_w(second_copy, 5 + 2 * s)
                 if s < 2:
                     load_w(12 + 2 * s)
                     load_w(13 + 2 * s)
@@ -305,18 +318,16 @@ def tile_bertselfattention_pa_l_kernel(tc, x, Wq, Wk, out):
                 sum_add(sg - 2)
             if has_combo(sg - 1) and vector_takes_last(sg - 1):
                 evac_proj(vcopy, sg - 1, 3)
-            if has_rows(sg - 2):
-                recip(sg - 2)
             if has_rows(sg - 1):
                 neg_max(sg - 1)
             if has_rows(sg - 2):
-                normalise_and_store(sg - 2)
+                recip(sg - 2)
             if has_combo(sg - 1):
-                quantize_qk(sg - 1)
+                merge_pairs(sg - 1)
+            if has_rows(sg - 2):
+                normalise_and_store(sg - 2)
             if head_w:
                 quantize_w(4 + 2 * s)
-            if s >= 6 and it + 1 < UNITS:
-                quantize_x(it + 1, s - 6)
 
             if has_combo(sg):
                 project(sg, 0)
@@ -329,6 +340,10 @@ def tile_bertselfattention_pa_l_kernel(tc, x, Wq, Wk, out):
             if has_rows(sg):
                 scores(sg)
                 row_max(sg)
+            if has_combo(sg - 1):
+                quantize_qk(sg - 1)
+            if s >= 6 and it + 1 < UNITS:
+                quantize_x(it + 1, s - 6)
             if has_combo(sg):
                 project(sg, 2)
                 project(sg, 3)

@@ -18,6 +18,7 @@ AXIS_X = mybir.AxisListType.X
 UNITS = B * H
 SLOTS = 8
 Q_MAT, K_MAT = 0, 1
+S_PIECES = (2, 6, 10, 11, 15)
 
 
 def unit_combos():
@@ -114,13 +115,12 @@ def tile_bertselfattention_pa_l_kernel(tc, x, Wq, Wk, out):
                 out=w_codes[pieces[i]][:].bitcast(FP8X4), scales=w_scales[pieces[i]][:], in_=w_grouped[i][:]
             )
 
-        def load_x(u):
+        def load_x(u, th):
             b, h = divmod(u, H)
-            raw = xraw_pool.tile([128, 4, D], BF16, name="xr")
+            if th == 0:
+                x_raw[u] = xraw_pool.tile([128, 4, D], BF16, name="xr")
             src = x[b, 512 * h : 512 * (h + 1), :].rearrange("(n p) d -> p n d", p=128)
-            for part in range(2):
-                nc.sync.dma_start(out=raw[:, 2 * part : 2 * part + 2, :], in_=src[:, 2 * part : 2 * part + 2, :])
-            x_raw[u] = raw
+            nc.sync.dma_start(out=x_raw[u][:, 2 * th : 2 * th + 2, :], in_=src[:, 2 * th : 2 * th + 2, :])
 
         def transpose_x(u, n):
             bank = ps1.tile([128, 512], F32, name="bank")
@@ -137,13 +137,15 @@ def tile_bertselfattention_pa_l_kernel(tc, x, Wq, Wk, out):
             dst = x_grouped[u][:].bitcast(F32).rearrange("p (g r w) -> p g r w", g=2, w=2)
             copy(out=dst[:, :, 128 * n : 128 * (n + 1), :], in_=bank[:].rearrange("p (g w r) -> p g r w", g=2, w=2))
 
-        def quantize_x(u, g):
-            x_codes[(u, g)] = xc_pool.tile([128, 512], U32, name="xc%d" % g, align_bytes=64)
-            x_scales[(u, g)] = xc_pool.tile([128, 512], U8, name="xs%d" % g, align_bytes=64)
+        def quantize_x(u, g, th):
+            if th == 0:
+                x_codes[(u, g)] = xc_pool.tile([128, 512], U32, name="xc%d" % g, align_bytes=64)
+                x_scales[(u, g)] = xc_pool.tile([128, 512], U8, name="xs%d" % g, align_bytes=64)
+            toks = slice(256 * th, 256 * (th + 1))
             nc.vector.quantize_mx(
-                out=x_codes[(u, g)][:].bitcast(FP8X4),
-                scales=x_scales[(u, g)][:],
-                in_=x_grouped[u][:, 2048 * g : 2048 * (g + 1)],
+                out=x_codes[(u, g)][:, toks].bitcast(FP8X4),
+                scales=x_scales[(u, g)][:, toks],
+                in_=x_grouped[u][:, 2048 * g + 1024 * th : 2048 * g + 1024 * (th + 1)],
             )
 
         def has_combo(sg):
@@ -271,90 +273,89 @@ def tile_bertselfattention_pa_l_kernel(tc, x, Wq, Wk, out):
         vcopy = nc.vector.tensor_copy
         scopy = nc.scalar.copy
 
-        def vector_takes_last(sg):
-            return sg >= SLOTS and sg % SLOTS < 6
+        def vector_takes_first(sg):
+            return sg >= SLOTS and sg % SLOTS not in (5, 6)
 
-        for i in range(2):
-            load_w(i)
-        load_x(0)
-        for i in range(2, 4):
-            load_w(i)
-        load_x(1)
+        def transpose_half(u, th):
+            first = transpose_x(u, 2 * th)
+            second = transpose_x(u, 2 * th + 1)
+            evac_x(scopy, u, 2 * th, first)
+            evac_x(scopy, u, 2 * th + 1, second)
+
+        load_w(0)
+        load_w(1)
+        load_x(0, 0)
+        load_w(2)
+        load_w(3)
+        load_x(0, 1)
         for i in range(4, 8):
             load_w(i)
+        load_x(1, 0)
+        load_x(1, 1)
 
         interleave_w(vcopy, 0)
         interleave_w(vcopy, 1)
-        for n0 in (0, 2):
-            first = transpose_x(0, n0)
-            second = transpose_x(0, n0 + 1)
-            evac_x(scopy, 0, n0, first)
-            evac_x(scopy, 0, n0 + 1, second)
+        transpose_half(0, 0)
         quantize_w(0)
         quantize_w(1)
-        interleave_w(scopy, 3)
-        quantize_x(0, 0)
-        quantize_x(0, 1)
-        interleave_w(vcopy, 2)
+        interleave_w(scopy, 2)
+        quantize_x(0, 0, 0)
+        quantize_x(0, 1, 0)
+        interleave_w(vcopy, 3)
+        transpose_half(0, 1)
         for i in range(8, 12):
             load_w(i)
-        quantize_w(3)
         quantize_w(2)
+        quantize_w(3)
+        quantize_x(0, 0, 1)
+        quantize_x(0, 1, 1)
 
-        for sg in range(SLOTS * (UNITS + 1) + 2):
+        for sg in range(SLOTS * (UNITS + 1) + 1):
             it, s = divmod(sg, SLOTS)
             head_w = it == 0 and s < 6
-            second_copy = scopy if s in (0, 2, 4) else vcopy
+            first_copy = vcopy if vector_takes_first(sg) else scopy
             if s == 0 and it + 2 < UNITS:
-                load_x(it + 2)
+                load_x(it + 2, 0)
+                load_x(it + 2, 1)
             if head_w:
-                interleave_w(vcopy, 4 + 2 * s)
-                interleave_w(second_copy, 5 + 2 * s)
+                for i in (4 + 2 * s, 5 + 2 * s):
+                    interleave_w(scopy if i in S_PIECES else vcopy, i)
                 if s < 2:
                     load_w(12 + 2 * s)
                     load_w(13 + 2 * s)
 
-            if has_rows(sg - 2):
-                sum_add(sg - 2)
-            if has_combo(sg - 1) and vector_takes_last(sg - 1):
-                evac_proj(vcopy, sg - 1, 3)
-            if has_rows(sg - 1):
-                neg_max(sg - 1)
-            if has_rows(sg - 2):
-                recip(sg - 2)
-            if has_combo(sg - 1):
-                merge_pairs(sg - 1)
-            if has_rows(sg - 2):
-                normalise_and_store(sg - 2)
-            if head_w:
-                quantize_w(4 + 2 * s)
-
-            if has_combo(sg):
-                project(sg, 0)
-                project(sg, 1)
-                evac_proj(scopy, sg, 0)
-            if has_rows(sg - 1):
-                exps(sg - 1)
-            if has_combo(sg):
-                evac_proj(scopy, sg, 1)
             if has_rows(sg):
                 scores(sg)
                 row_max(sg)
-            if has_combo(sg - 1):
-                quantize_qk(sg - 1)
-            if s >= 6 and it + 1 < UNITS:
-                quantize_x(it + 1, s - 6)
+            if has_combo(sg):
+                project(sg, 0)
+                evac_proj(first_copy, sg, 0)
+            if has_rows(sg):
+                neg_max(sg)
+            if has_combo(sg):
+                project(sg, 1)
+                evac_proj(scopy, sg, 1)
+            if has_rows(sg):
+                exps(sg)
             if has_combo(sg):
                 project(sg, 2)
                 project(sg, 3)
                 evac_proj(scopy, sg, 2)
-                if not vector_takes_last(sg):
-                    evac_proj(scopy, sg, 3)
+                evac_proj(scopy, sg, 3)
+            if head_w:
+                quantize_w(4 + 2 * s)
+            if has_combo(sg - 1):
+                merge_pairs(sg - 1)
+            if has_rows(sg - 1):
+                sum_add(sg - 1)
+            if s in (2, 3, 5, 6) and it + 1 < UNITS:
+                quantize_x(it + 1, (s - 2) % 3, (s - 2) // 3)
+            if has_combo(sg - 1):
+                quantize_qk(sg - 1)
+            if has_rows(sg - 1):
+                recip(sg - 1)
+                normalise_and_store(sg - 1)
             if s in (1, 4) and it + 1 < UNITS:
-                n0 = 0 if s == 1 else 2
-                first = transpose_x(it + 1, n0)
-                second = transpose_x(it + 1, n0 + 1)
-                evac_x(scopy, it + 1, n0, first)
-                evac_x(scopy, it + 1, n0 + 1, second)
+                transpose_half(it + 1, s // 4)
             if head_w:
                 quantize_w(5 + 2 * s)

@@ -274,7 +274,7 @@ def tile_bertselfattention_pa_l_kernel(tc, x, Wq, Wk, out):
         scopy = nc.scalar.copy
 
         def vector_takes_first(sg):
-            return sg >= SLOTS and sg % SLOTS not in (5, 6)
+            return sg >= SLOTS and sg % SLOTS not in (4, 7)
 
         def transpose_half(u, th):
             first = transpose_x(u, 2 * th)

from contextlib import ExitStack

import concourse.mybir as mybir
from concourse.masks import make_identity

B, S, D, H = 8, 1024, 1024, 2
FLOPS = 2 * B * S * D * (2 * H * D) + 2 * B * H * S * S * D

F32 = mybir.dt.float32
BF16 = mybir.dt.bfloat16
U32 = mybir.dt.uint32
U8 = mybir.dt.uint8
FP8X4 = mybir.dt.float8_e4m3fn_x4
ALU = mybir.AluOpType
ACT = mybir.ActivationFunctionType
AXIS_X = mybir.AxisListType.X

UNITS = B * H
SLOTS = 8
Q_MAT, K_MAT = 0, 1
S_PIECES = (2, 6, 10, 11, 15)


def unit_combos():
    combos = []
    for g in range(2):
        for tb in range(2):
            banks = [(2 * half + g, a, 256 * tb, 256 * half) for half in range(2) for a in range(2)]
            combos.append((K_MAT, g, tb, banks))
    for hq in range(2):
        for g in range(2):
            banks = [(2 * hq + g, a, 256 * th, 256 * th) for th in range(2) for a in range(2)]
            combos.append((Q_MAT, g, hq, banks))
    return combos


def weight_pieces():
    pieces = []
    for grp in (0, 2, 1, 3):
        for kp in range(2):
            pieces.append((K_MAT, grp, kp))
    for grp in range(4):
        for kp in range(2):
            pieces.append((Q_MAT, grp, kp))
    return pieces


def tile_bertselfattention_pa_l_kernel(tc, x, Wq, Wk, out):
    nc = tc.nc
    weights = (Wq, Wk)
    combos = unit_combos()
    pieces = weight_pieces()

    with ExitStack() as ctx:
        keep = ctx.enter_context(tc.tile_pool(name="keep", bufs=1))
        wraw_pool = ctx.enter_context(tc.tile_pool(name="wraw", bufs=8))
        xraw_pool = ctx.enter_context(tc.tile_pool(name="xraw", bufs=2))
        xg_pool = ctx.enter_context(tc.tile_pool(name="xg", bufs=2))
        xc_pool = ctx.enter_context(tc.tile_pool(name="xc", bufs=2))
        gr_pool = ctx.enter_context(tc.tile_pool(name="gr", bufs=4))
        hg_pool = ctx.enter_context(tc.tile_pool(name="hg", bufs=4))
        qk_pool = ctx.enter_context(tc.tile_pool(name="qk", bufs=2))
        e_pool = ctx.enter_context(tc.tile_pool(name="e", bufs=4))
        o_pool = ctx.enter_context(tc.tile_pool(name="o", bufs=4))
        st_pool = ctx.enter_context(tc.tile_pool(name="st", bufs=6))
        ps1 = ctx.enter_context(tc.psum_pool(name="ps1", bufs=4))
        ps2 = ctx.enter_context(tc.psum_pool(name="ps2", bufs=4))
        ctx.enter_context(tc.manual_schedule())

        ident = keep.tile([128, 128], F32, name="ident")
        make_identity(nc, ident[:])
        warm_in = keep.tile([128, 1], F32, name="warm_in")
        warm_out = keep.tile([128, 1], F32, name="warm_out")
        nc.vector.memset(warm_in[:], 0.0)
        nc.scalar.activation(out=warm_out[:], in_=warm_in[:], func=ACT.Exp)

        w_codes = {}
        w_scales = {}
        for piece in pieces:
            w_codes[piece] = keep.tile([128, 512], U32, name="wc%d%d%d" % piece, align_bytes=64)
            w_scales[piece] = keep.tile([128, 512], U8, name="ws%d%d%d" % piece, align_bytes=64)

        w_raw = {}
        w_grouped = {}
        x_raw = {}
        x_grouped = {}
        x_codes = {}
        x_scales = {}
        qk_codes = {}
        qk_scales = {}
        banks_of = {}
        grouped_of = {}
        halves_of = {}
        scores_of = {}
        stats_of = {}
        exp_of = {}

        def load_w(i):
            m, grp, kp = pieces[i]
            raw = wraw_pool.tile([128, 4, 512], BF16, name="wr")
            src = weights[m][512 * kp : 512 * (kp + 1), 512 * grp : 512 * (grp + 1)]
            nc.sync.dma_start(out=raw[:], in_=src.rearrange("(p j) c -> p j c", j=4))
            w_raw[i] = raw

        def interleave_w(copy, i):
            grouped = gr_pool.tile([128, 2048], BF16, name="gr", align_bytes=64)
            copy(
                out=grouped[:].rearrange("p (t m j) -> p t m j", t=4, j=4),
                in_=w_raw[i][:].rearrange("p j (m t) -> p t m j", t=4),
            )
            w_grouped[i] = grouped

        def quantize_w(i):
            nc.vector.quantize_mx(
                out=w_codes[pieces[i]][:].bitcast(FP8X4), scales=w_scales[pieces[i]][:], in_=w_grouped[i][:]
            )

        def load_x(u, th):
            b, h = divmod(u, H)
            if th == 0:
                x_raw[u] = xraw_pool.tile([128, 4, D], BF16, name="xr")
            src = x[b, 512 * h : 512 * (h + 1), :].rearrange("(n p) d -> p n d", p=128)
            nc.sync.dma_start(out=x_raw[u][:, 2 * th : 2 * th + 2, :], in_=src[:, 2 * th : 2 * th + 2, :])

        def transpose_x(u, n):
            bank = ps1.tile([128, 512], F32, name="bank")
            words = x_raw[u][:, n, :].bitcast(F32)
            for g in range(2):
                for w in range(2):
                    c0 = 128 * (2 * g + w)
                    nc.tensor.transpose(bank[:, c0 : c0 + 128], words[:, 256 * g + w : 256 * (g + 1) : 2], ident[:])
            return bank

        def evac_x(copy, u, n, bank):
            if n == 0:
                x_grouped[u] = xg_pool.tile([128, 4096], BF16, name="xg", align_bytes=64)
            dst = x_grouped[u][:].bitcast(F32).rearrange("p (g r w) -> p g r w", g=2, w=2)
            copy(out=dst[:, :, 128 * n : 128 * (n + 1), :], in_=bank[:].rearrange("p (g w r) -> p g r w", g=2, w=2))

        def quantize_x(u, g, th):
            if th == 0:
                x_codes[(u, g)] = xc_pool.tile([128, 512], U32, name="xc%d" % g, align_bytes=64)
                x_scales[(u, g)] = xc_pool.tile([128, 512], U8, name="xs%d" % g, align_bytes=64)
            toks = slice(256 * th, 256 * (th + 1))
            nc.vector.quantize_mx(
                out=x_codes[(u, g)][:, toks].bitcast(FP8X4),
                scales=x_scales[(u, g)][:, toks],
                in_=x_grouped[u][:, 2048 * g + 1024 * th : 2048 * g + 1024 * (th + 1)],
            )

        def has_combo(sg):
            return 0 <= sg < SLOTS * UNITS

        def project(sg, k):
            u, s = divmod(sg, SLOTS)
            m, g, part, banks = combos[s]
            grp, a, tok0, off = banks[k]
            bank = ps1.tile([128, 512], F32, name="bank")
            toks = slice(tok0, tok0 + 256)
            for w in range(2):
                cols = slice(128 * (2 * a + w), 128 * (2 * a + w + 1))
                for kp in range(2):
                    nc.tensor.matmul_mx(
                        out=bank[:, 256 * w : 256 * (w + 1)],
                        lhsT=w_codes[(m, grp, kp)][:, cols].bitcast(FP8X4),
                        lhsT_scale=w_scales[(m, grp, kp)][:, cols],
                        rhs=x_codes[(u, kp)][:, toks].bitcast(FP8X4),
                        rhs_scale=x_scales[(u, kp)][:, toks],
                        start=(kp == 0),
                        stop=(kp == 1),
                    )
            banks_of[(sg, k)] = bank

        def evac_proj(copy, sg, k):
            grp, a, tok0, off = combos[sg % SLOTS][3][k]
            if k == 0:
                halves_of[sg] = hg_pool.tile([128, 2048], BF16, name="hg", align_bytes=64)
            c0 = 1024 * a + 2 * off
            copy(
                out=halves_of[sg][:, c0 : c0 + 512].rearrange("p (r w) -> p r w", w=2),
                in_=banks_of[(sg, k)][:].rearrange("p (w r) -> p r w", w=2),
            )

        def merge_pairs(sg):
            grouped_of[sg] = gr_pool.tile([128, 2048], BF16, name="gr", align_bytes=64)
            nc.vector.tensor_copy(
                out=grouped_of[sg][:].bitcast(F32).rearrange("p (c a) -> p c a", a=2),
                in_=halves_of[sg][:].bitcast(F32).rearrange("p (a c) -> p c a", a=2),
            )

        def quantize_qk(sg):
            u, s = divmod(sg, SLOTS)
            m, g, part, banks = combos[s]
            key = (u, m, g, part)
            qk_codes[key] = qk_pool.tile([128, 512], U32, name="qkc%d%d%d" % (m, g, part), align_bytes=64)
            qk_scales[key] = qk_pool.tile([128, 512], U8, name="qks%d%d%d" % (m, g, part), align_bytes=64)
            nc.vector.quantize_mx(out=qk_codes[key][:].bitcast(FP8X4), scales=qk_scales[key][:], in_=grouped_of[sg][:])

        def has_rows(sg):
            return SLOTS <= sg < SLOTS * (UNITS + 1)

        def scores(sg):
            u, s = divmod(sg - SLOTS, SLOTS)
            hq, tq = divmod(s, 4)
            rows = slice(128 * tq, 128 * (tq + 1))
            pair = []
            for tb in range(2):
                ps = ps2.tile([128, 512], F32, name="sc")
                for g in range(2):
                    nc.tensor.matmul_mx(
                        out=ps[:],
                        lhsT=qk_codes[(u, Q_MAT, g, hq)][:, rows].bitcast(FP8X4),
                        lhsT_scale=qk_scales[(u, Q_MAT, g, hq)][:, rows],
                        rhs=qk_codes[(u, K_MAT, g, tb)][:].bitcast(FP8X4),
                        rhs_scale=qk_scales[(u, K_MAT, g, tb)][:],
                        start=(g == 0),
                        stop=(g == 1),
                    )
                pair.append(ps)
            scores_of[sg] = pair

        def row_max(sg):
            mx = st_pool.tile([128, 2], F32, name="mx")
            for tb in range(2):
                nc.vector.tensor_reduce(out=mx[:, tb : tb + 1], in_=scores_of[sg][tb][:], axis=AXIS_X, op=ALU.max)
            stats_of[(sg, "mx")] = mx

        def neg_max(sg):
            mx = stats_of[(sg, "mx")]
            nb = st_pool.tile([128, 1], F32, name="nb")
            nc.vector.tensor_scalar(
                out=nb[:], in0=mx[:, 0:1], scalar1=mx[:, 1:2], scalar2=-1.0 / 32.0, op0=ALU.max, op1=ALU.mult
            )
            stats_of[(sg, "nb")] = nb

        def exps(sg):
            e = e_pool.tile([128, 1024], F32, name="e")
            ss = st_pool.tile([128, 2], F32, name="ss")
            for tb in range(2):
                nc.scalar.activation(
                    out=e[:, 512 * tb : 512 * (tb + 1)].rearrange("p (t h) -> p t h", h=2),
                    in_=scores_of[sg][tb][:].rearrange("p (h t) -> p t h", h=2),
                    func=ACT.Exp,
                    bias=stats_of[(sg, "nb")][:],
                    scale=1.0 / 32.0,
                    accum_out=ss[:, tb : tb + 1],
                )
            exp_of[sg] = e
            stats_of[(sg, "ss")] = ss

        def sum_add(sg):
            ss = stats_of[(sg, "ss")]
            tot = st_pool.tile([128, 1], F32, name="tot")
            nc.vector.tensor_tensor(out=tot[:], in0=ss[:, 0:1], in1=ss[:, 1:2], op=ALU.add)
            stats_of[(sg, "tot")] = tot

        def recip(sg):
            rc = st_pool.tile([128, 1], F32, name="rc")
            nc.vector.reciprocal(out=rc[:], in_=stats_of[(sg, "tot")][:])
            stats_of[(sg, "rc")] = rc

        def normalise_and_store(sg):
            u, s = divmod(sg - SLOTS, SLOTS)
            b, h = divmod(u, H)
            hq, tq = divmod(s, 4)
            o = o_pool.tile([128, 1024], F32, name="o")
            nc.gpsimd.tensor_scalar(
                out=o[:], in0=exp_of[sg][:], scalar1=stats_of[(sg, "rc")][:], scalar2=1.0, op0=ALU.mult, op1=ALU.mult
            )
            dst = out[b, h].rearrange("(t two) j -> two t j", two=2)
            nc.sync.dma_start(out=dst[hq, 128 * tq : 128 * (tq + 1), :], in_=o[:])

        vcopy = nc.vector.tensor_copy
        scopy = nc.scalar.copy

        def vector_takes_first(sg):
            return sg >= SLOTS and sg % SLOTS not in (4, 7)

        def transpose_half(u, th):
            first = transpose_x(u, 2 * th)
            second = transpose_x(u, 2 * th + 1)
            evac_x(scopy, u, 2 * th, first)
            evac_x(scopy, u, 2 * th + 1, second)

        load_w(0)
        load_w(1)
        load_x(0, 0)
        load_w(2)
        load_w(3)
        load_x(0, 1)
        for i in range(4, 8):
            load_w(i)
        load_x(1, 0)
        load_x(1, 1)

        interleave_w(vcopy, 0)
        interleave_w(vcopy, 1)
        transpose_half(0, 0)
        quantize_w(0)
        quantize_w(1)
        interleave_w(scopy, 2)
        quantize_x(0, 0, 0)
        quantize_x(0, 1, 0)
        interleave_w(vcopy, 3)
        transpose_half(0, 1)
        for i in range(8, 12):
            load_w(i)
        quantize_w(2)
        quantize_w(3)
        quantize_x(0, 0, 1)
        quantize_x(0, 1, 1)

        for sg in range(SLOTS * (UNITS + 1) + 1):
            it, s = divmod(sg, SLOTS)
            head_w = it == 0 and s < 6
            first_copy = vcopy if vector_takes_first(sg) else scopy
            if s == 0 and it + 2 < UNITS:
                load_x(it + 2, 0)
                load_x(it + 2, 1)
            if head_w:
                for i in (4 + 2 * s, 5 + 2 * s):
                    interleave_w(scopy if i in S_PIECES else vcopy, i)
                if s < 2:
                    load_w(12 + 2 * s)
                    load_w(13 + 2 * s)

            if has_rows(sg):
                scores(sg)
                row_max(sg)
            if has_combo(sg):
                project(sg, 0)
                evac_proj(first_copy, sg, 0)
            if has_rows(sg):
                neg_max(sg)
            if has_combo(sg):
                project(sg, 1)
                evac_proj(scopy, sg, 1)
            if has_rows(sg):
                exps(sg)
            if has_combo(sg):
                project(sg, 2)
                project(sg, 3)
                evac_proj(scopy, sg, 2)
                evac_proj(scopy, sg, 3)
            if head_w:
                quantize_w(4 + 2 * s)
            if has_combo(sg - 1):
                merge_pairs(sg - 1)
            if has_rows(sg - 1):
                sum_add(sg - 1)
            if s in (2, 3, 5, 6) and it + 1 < UNITS:
                quantize_x(it + 1, (s - 2) % 3, (s - 2) // 3)
            if has_combo(sg - 1):
                quantize_qk(sg - 1)
            if has_rows(sg - 1):
                recip(sg - 1)
                normalise_and_store(sg - 1)
            if s in (1, 4) and it + 1 < UNITS:
                transpose_half(it + 1, s // 4)
            if head_w:
                quantize_w(5 + 2 * s)
